import numpy as np
import ml_dtypes


def mxq(x, axis, fmt="e4m3"):
    dtype, down = {"e4m3": (ml_dtypes.float8_e4m3fn, 7), "e5m2": (ml_dtypes.float8_e5m2, 14)}[fmt]
    v = np.moveaxis(np.asarray(x, np.float32).astype(ml_dtypes.bfloat16).astype(np.float64), axis, -1)
    blocks = v.reshape(v.shape[:-1] + (-1, 32))
    amax = np.abs(blocks).max(-1, keepdims=True)
    byte = np.maximum(np.where(amax > 0, np.frexp(amax)[1] - 1 + 127, 0) - down, 1)
    scale = np.exp2(byte - 127.0)
    codes = (blocks / scale).astype(np.float32).astype(dtype).astype(np.float64)
    return np.moveaxis((codes * scale).reshape(v.shape), -1, axis)


WIDE = False


def mx_kscale(k):
    if not WIDE:
        return np.ones(k)
    levels = np.array([10, -10, 5, -5, 0])
    if k % 512:
        return np.exp2(np.random.permutation(np.resize(levels, k // 32))).repeat(32)
    a = np.empty((k // 512, 16))
    for p in range(k // 512):
        a[p, :8] = np.random.permutation(np.resize(levels, 8))
        for g in range(8):
            far = levels[np.abs(levels - a[p, g]) >= 10]
            a[p, g + 8] = far[np.random.randint(len(far))]
    return np.exp2(a.ravel()).repeat(32)


BF16 = ml_dtypes.bfloat16


def bf(x):
    return np.asarray(x, np.float32).astype(BF16)


def f64(x):
    return np.asarray(x).astype(np.float64)


B, CIN, CK, CV, COUT, H, W, KS, DA, DB, DC = 2, 2048, 2048, 2048, 2048, 64, 64, 3, 1, 2, 4
DILS = (DA, DB, DC)
NN = KS * KS * len(DILS)
P = H * W


def rn(*shape):
    return np.random.standard_normal(shape)


def shifted(a, d, i, j):
    ap = np.pad(a, ((0, 0), (0, 0), (d, d), (d, d)))
    return ap[:, :, i * d:i * d + H, j * d:j * d + W]


def setup_inputs():
    s, t = mx_kscale(CIN), mx_kscale(CV)
    z = 1.2 * rn(B, NN, H, W)
    e = np.exp(z - z.max(axis=1, keepdims=True))
    return {"x": bf(rn(B, CIN, H, W) * s[None, :, None, None]),
            "attn": bf(e / e.sum(axis=1, keepdims=True)),
            "v_w": bf(rn(CV, CIN) / np.sqrt(CIN) / s[None, :] * t[:, None]),
            "v_b": bf(0.2 * rn(CV) * t),
            "w_w": bf(rn(COUT, CV) * 1.5 / np.sqrt(CV) / t[None, :]),
            "w_b": bf(0.3 * rn(COUT))}


def reference(x, attn, v_w, v_b, w_w, w_b):
    value = (mxq(f64(v_w), 1, "e4m3") @ mxq(f64(x).reshape(B, CIN, P), 1, "e4m3")) + f64(v_b)[None, :, None]
    vf = value.reshape(B, CV, H, W)
    a = f64(attn)
    offs = [(d, i, j) for d in DILS for i in range(KS) for j in range(KS)]
    context = sum(a[:, n:n + 1] * shifted(vf, d, i, j) for n, (d, i, j) in enumerate(offs))
    out = (mxq(f64(w_w), 1, "e4m3") @ mxq(context.reshape(B, CV, P), 1, "e4m3")) + f64(w_b)[None, :, None]
    return out.reshape(B, COUT, H, W)

@@ -1,0 +1,383 @@
+from contextlib import ExitStack
+
+import concourse.mybir as mybir
+from concourse.masks import make_identity
+
+FLOPS = 2 * 2 * 2048 * 2048 * 8192 + 2 * 27 * 2048 * 8192
+
+F32 = mybir.dt.float32
+BF16 = mybir.dt.bfloat16
+U32 = mybir.dt.uint32
+U8 = mybir.dt.uint8
+FP8X4 = mybir.dt.float8_e4m3fn_x4
+ADD = mybir.AluOpType.add
+MULT = mybir.AluOpType.mult
+IDENTITY = mybir.ActivationFunctionType.Identity
+
+P = 128
+IMG = 64
+TR = 8
+TCOL = 16
+HALO = 4
+STRIPES = 16
+NTAP = 27
+
+
+def tap_offsets():
+    taps = []
+    for n in range(NTAP):
+        d = (1, 2, 4)[n // 9]
+        dr = ((n % 9) // 3 - 1) * d
+        dc = (n % 3 - 1) * d
+        taps.append((n, dr, dc))
+    return taps
+
+
+def band_plan(gam):
+    written = [[False] * IMG for r in range(TR)]
+    parts = []
+    if gam >= 0:
+        parts.append((gam, 1, 0, 4 if gam % 8 == 7 else 8))
+    if gam + 1 < STRIPES:
+        parts.append((gam + 1, 0, 4 if (gam + 1) % 8 == 0 else 0, 8))
+    pieces = []
+    for (sg, half, r0, r1) in parts:
+        for s in range(4):
+            lo = max(0, TCOL * s - HALO)
+            hi = min(IMG, TCOL * s + TCOL + HALO)
+            first = lo
+            for c in range(lo + 1, hi + 1):
+                if c == hi or written[r0][c] != written[r0][first]:
+                    pieces.append((sg, s, half, r0, r1, first, c))
+                    first = c
+            for r in range(r0, r1):
+                for cc in range(lo, hi):
+                    written[r][cc] = True
+    return pieces
+
+
+def prep_weight(nc, wst, pst, ident, w, permute, codes, planes):
+    for cg in range(4):
+        rows = w[512 * cg : 512 * (cg + 1), :]
+        wr = wst.tile([P, 4, 2048], BF16, name="wr", tag="wr")
+        if permute:
+            nc.sync.dma_start(out=wr[:], in_=rows.rearrange("(m t) k -> m t k", t=4))
+        else:
+            nc.sync.dma_start(out=wr[:], in_=rows.rearrange("(t m) k -> m t k", t=4))
+        words = wr[:].bitcast(F32)
+        for g in range(4):
+            grp = wst.tile([P, 512, 4], BF16, name="wg", tag="wg", align_bytes=64)
+            flat = grp[:].rearrange("p c j -> p (c j)")
+            gw = flat.bitcast(F32)
+            for h in range(2):
+                pt = pst.tile([P, 2, 2, P], F32, name="pt", tag="pt")
+                for tt in range(2):
+                    for u in range(2):
+                        nc.tensor.transpose(
+                            pt[:, tt, u, :],
+                            words[:, 2 * h + tt, 256 * g + u : 256 * (g + 1) : 2],
+                            ident[:],
+                        )
+                dst = gw[:, 512 * h : 512 * (h + 1)].rearrange("p (t m u) -> p t m u", t=2, u=2)
+                src = pt[:].rearrange("p t u m -> p t m u")
+                if h == 0:
+                    nc.vector.tensor_copy(out=dst, in_=src)
+                else:
+                    nc.scalar.copy(out=dst, in_=src)
+            cols = slice(512 * cg, 512 * (cg + 1))
+            nc.vector.quantize_mx(
+                out=codes[:, g, cols].bitcast(FP8X4),
+                scales=planes[4 * g : P, cols],
+                in_=flat,
+            )
+
+
+def prep_small(nc, pro, pst, ident, attn, v_b, w_b, taps, vbb, wbc):
+    ash = pro.tile([P, 2, IMG, IMG], BF16, name="ash")
+    nc.vector.memset(ash[:], 0.0)
+    for (n, dr, dc) in tap_offsets():
+        r0, r1 = max(0, dr), min(IMG, IMG + dr)
+        c0, c1 = max(0, dc), min(IMG, IMG + dc)
+        for b in range(2):
+            nc.scalar.dma_start(
+                out=ash[n : n + 1, b, r0:r1, c0:c1],
+                in_=attn[b, n : n + 1, r0 - dr : r1 - dr, c0 - dc : c1 - dc],
+            )
+    asp = pro.tile([P, 64, P], F32, name="asp")
+    for sg in range(STRIPES):
+        b, j = divmod(sg, 8)
+        nc.vector.tensor_copy(
+            out=asp[:, 4 * sg : 4 * sg + 4, :].rearrange("p s (r c) -> p s r c", c=TCOL),
+            in_=ash[:, b, TR * j : TR * (j + 1), :].rearrange("p r (s c) -> p s r c", c=TCOL),
+        )
+    for k in range(16):
+        pt = pst.tile([P, 4, P], F32, name="pt", tag="pt")
+        for i in range(4):
+            nc.tensor.transpose(pt[:, i, :], asp[:, 4 * k + i, :], ident[:])
+        nc.vector.tensor_copy(out=taps[:, 4 * k : 4 * k + 4, :], in_=pt[:, :, 0:NTAP])
+    nc.vector.tensor_tensor(out=taps[:, :, 4], in0=taps[:, :, 4], in1=taps[:, :, 13], op=ADD)
+    nc.vector.tensor_tensor(out=taps[:, :, 4], in0=taps[:, :, 4], in1=taps[:, :, 22], op=ADD)
+
+    vbr = pro.tile([P, 2048], BF16, name="vbr")
+    nc.sync.dma_start(out=vbr[:], in_=v_b.partition_broadcast(P))
+    nc.vector.tensor_copy(
+        out=vbb[:].rearrange("p (g t m) -> p g t m", g=4, t=4),
+        in_=vbr[:].rearrange("p (g m t) -> p g t m", g=4, t=4),
+    )
+
+    wbr = pro.tile([P, P], BF16, name="wbr")
+    nc.vector.memset(wbr[:], 0.0)
+    nc.sync.dma_start(out=wbr[0:16, :], in_=w_b.rearrange("(a m) -> a m", m=P))
+    wbf = pro.tile([P, P], F32, name="wbf")
+    nc.vector.tensor_copy(out=wbf[:], in_=wbr[:])
+    pt = pst.tile([P, 4, P], F32, name="pt", tag="pt")
+    nc.tensor.transpose(pt[:, 0, :], wbf[:], ident[:])
+    nc.vector.tensor_copy(out=wbc[:], in_=pt[:, 0, 0:16])
+
+
+def tile_selfattentionmodulev2_pb_l_kernel(tc, x, attn, v_w, v_b, w_w, w_b, out):
+    nc = tc.nc
+    with ExitStack() as ctx:
+        const = ctx.enter_context(tc.tile_pool(name="const", bufs=1))
+        xrp = ctx.enter_context(tc.tile_pool(name="xrp", bufs=4))
+        xgp = ctx.enter_context(tc.tile_pool(name="xgp", bufs=2))
+        xcp = ctx.enter_context(tc.tile_pool(name="xcp", bufs=1))
+
+        ident = const.tile([P, P], F32, name="ident")
+        make_identity(nc, ident[:])
+        vwc = const.tile([P, 4, 2048], U32, name="vwc", align_bytes=64)
+        vws = const.tile([P, 2048], U8, name="vws", align_bytes=64)
+        wwc = const.tile([P, 4, 2048], U32, name="wwc", align_bytes=64)
+        wws = const.tile([P, 2048], U8, name="wws", align_bytes=64)
+        taps = const.tile([P, 64, NTAP], F32, name="taps")
+        vbb = const.tile([P, 2048], F32, name="vbb")
+        wbc = const.tile([P, 16], F32, name="wbc")
+
+        xraw = {}
+        xgrp = {}
+        xcod = {}
+        vts = {}
+        ats = {}
+
+        def load_x(sg, g):
+            b, j = divmod(sg, 8)
+            xr = xrp.tile([P, 4, 512], BF16, name="xr", tag="xr")
+            nc.sync.dma_start(
+                out=xr[:],
+                in_=x[b, 512 * g : 512 * (g + 1), TR * j : TR * (j + 1), :].rearrange(
+                    "(p i) h w -> p i (h w)", i=4
+                ),
+            )
+            xraw[(sg, g)] = xr
+
+        def x_codes(sg):
+            xc = xcp.tile([P, 4, 512], U32, name="xc", tag="xc", align_bytes=64)
+            xs = xcp.tile([P, 512], U8, name="xs", tag="xs", align_bytes=64)
+            xcod[sg] = (xc, xs)
+
+        def x_copy(sg, g, s):
+            if s == 0:
+                xgrp[(sg, g)] = xgp.tile([P, 512, 4], BF16, name="xg", tag="xg", align_bytes=64)
+            xg = xgrp[(sg, g)]
+            xr = xraw[(sg, g)]
+            nc.scalar.copy(
+                out=xg[:, P * s : P * (s + 1), :].rearrange("p (r c) i -> p r c i", c=TCOL),
+                in_=xr[:].rearrange("p i (r s c) -> p s r c i", s=4, c=TCOL)[:, s],
+            )
+
+        def x_quant(sg, g):
+            xc, xs = xcod[sg]
+            nc.vector.quantize_mx(
+                out=xc[:, g, :].bitcast(FP8X4),
+                scales=xs[4 * g : P, :],
+                in_=xgrp[(sg, g)][:].rearrange("p c i -> p (c i)"),
+            )
+
+        with tc.tile_pool(name="pro", bufs=1) as pro:
+            with tc.tile_pool(name="wst", bufs=2) as wst:
+                with tc.psum_pool(name="pst", bufs=4) as pst:
+                    prep_small(nc, pro, pst, ident, attn, v_b, w_b, taps, vbb, wbc)
+                    prep_weight(nc, wst, pst, ident, v_w, True, vwc, vws)
+                    for g in range(4):
+                        load_x(0, g)
+                    prep_weight(nc, wst, pst, ident, w_w, False, wwc, wws)
+
+        vtp = ctx.enter_context(tc.tile_pool(name="vtp", bufs=8))
+        atp = ctx.enter_context(tc.tile_pool(name="atp", bufs=12))
+        cbp = ctx.enter_context(tc.tile_pool(name="cbp", bufs=2))
+        cgp = ctx.enter_context(tc.tile_pool(name="cgp", bufs=2))
+        ccp = ctx.enter_context(tc.tile_pool(name="ccp", bufs=1))
+        obp = ctx.enter_context(tc.tile_pool(name="obp", bufs=4))
+        ps1 = ctx.enter_context(tc.psum_pool(name="ps1", bufs=3))
+        psb = ctx.enter_context(tc.psum_pool(name="psb", bufs=2))
+        ps2 = ctx.enter_context(tc.psum_pool(name="ps2", bufs=3))
+
+        a_ops = [(n, dr, dc, s) for (n, dr, dc) in tap_offsets() if n != 13 and n != 22 for s in range(4)]
+        ident3 = ident[:].rearrange("p (r c) -> p r c", c=TCOL)
+
+        def a_init(sg):
+            for s in range(4):
+                at = atp.tile([P, 2 * TR, TCOL + 2 * HALO], F32, name="at", tag="at")
+                nc.gpsimd.memset(at[:], 0.0)
+                ats[(sg, s)] = at
+
+        def a_op(sg, k):
+            n, dr, dc, s = a_ops[k]
+            at = ats[(sg, s)]
+            win = at[:, HALO - dr : HALO - dr + TR, HALO - dc : HALO - dc + TCOL]
+            nc.vector.scalar_tensor_tensor(
+                out=win,
+                in0=ident3,
+                scalar=taps[:, 4 * sg + s, n : n + 1],
+                in1=win,
+                op0=MULT,
+                op1=ADD,
+            )
+
+        def stage1(sg):
+            xc, xs = xcod[sg]
+            for s in range(4):
+                vt = vtp.tile([P, 2048], F32, name="vt", tag="vt")
+                vts[(sg, s)] = vt
+                px = slice(P * s, P * (s + 1))
+                for cg in range(4):
+                    cols = slice(512 * cg, 512 * (cg + 1))
+                    ps = ps1.tile([P, 512], F32, name="s1", tag="s1")
+                    for g in range(4):
+                        nc.tensor.matmul_mx(
+                            out=ps[:],
+                            lhsT=xc[:, g, px].bitcast(FP8X4),
+                            lhsT_scale=xs[4 * g : P, px],
+                            rhs=vwc[:, g, cols].bitcast(FP8X4),
+                            rhs_scale=vws[4 * g : P, cols],
+                            start=(g == 0),
+                            stop=(g == 3),
+                        )
+                    nc.vector.tensor_tensor(out=vt[:, cols], in0=ps[:], in1=vbb[:, cols], op=ADD)
+
+        def banded(plan, ct, cb, px):
+            ps = psb.tile([P, TR, IMG], F32, name="bd", tag="bd")
+            last = len(plan) - 1
+            for i, (sg, s, half, r0, r1, c0, c1) in enumerate(plan):
+                a0 = TCOL * s - HALO
+                nc.tensor.matmul(
+                    out=ps[:, r0:r1, c0:c1],
+                    lhsT=vts[(sg, s)][:, P * ct : P * (ct + 1)],
+                    rhs=ats[(sg, s)][:, TR * half + r0 : TR * half + r1, c0 - a0 : c1 - a0],
+                    start=(i == 0),
+                    stop=(i == last),
+                )
+            nc.scalar.copy(out=cb[:, ct % 4, px], in_=ps[:].rearrange("p r c -> p (r c)")[:, px])
+
+        def store(gam, ot, ob):
+            orow = slice(P * ot, P * (ot + 1))
+            if gam >= 0 and gam % 8 != 7:
+                b, j = divmod(gam, 8)
+                nc.sync.dma_start(
+                    out=out[b, orow, TR * j + 4 : TR * j + 12, :].rearrange("o h w -> o (h w)"),
+                    in_=ob[:],
+                )
+            else:
+                if gam >= 0:
+                    nc.sync.dma_start(
+                        out=out[gam // 8, orow, IMG - 4 : IMG, :].rearrange("o h w -> o (h w)"),
+                        in_=ob[:, 0:256],
+                    )
+                if gam + 1 < STRIPES:
+                    nc.sync.dma_start(
+                        out=out[(gam + 1) // 8, orow, 0:4, :].rearrange("o h w -> o (h w)"),
+                        in_=ob[:, 256:512],
+                    )
+
+        def stage2(gam, ot, cc, cs, px):
+            ps = ps2.tile([P, 512], F32, name="s2", tag="s2")
+            ocol = slice(P * ot, P * (ot + 1))
+            for g in range(4):
+                nc.tensor.matmul_mx(
+                    out=ps[:, px],
+                    lhsT=wwc[:, g, ocol].bitcast(FP8X4),
+                    lhsT_scale=wws[4 * g : P, ocol],
+                    rhs=cc[:, g, px].bitcast(FP8X4),
+                    rhs_scale=cs[4 * g : P, px],
+                    start=(g == 0),
+                    stop=(g == 3),
+                )
+            ob = obp.tile([P, 512], F32, name="ob", tag="ob")
+            nc.scalar.activation(
+                out=ob[:, px], in_=ps[:, px], func=IDENTITY, bias=wbc[:, ot : ot + 1], scale=1.0
+            )
+            store(gam, ot, ob)
+
+        ctx.enter_context(tc.manual_schedule())
+
+        x_codes(0)
+        for g in range(4):
+            for s in range(4):
+                x_copy(0, g, s)
+            x_quant(0, g)
+            load_x(1, g)
+        a_init(0)
+        for k in range(len(a_ops)):
+            a_op(0, k)
+        stage1(0)
+
+        for gam in range(-1, STRIPES):
+            nxt = gam + 2
+            have = nxt < STRIPES
+            plan = band_plan(gam)
+            px = slice(256 if gam < 0 else 0, 256 if gam == STRIPES - 1 else 512)
+            cc = ccp.tile([P, 4, 512], U32, name="cc", tag="cc", align_bytes=64)
+            cs = ccp.tile([P, 512], U8, name="cs", tag="cs", align_bytes=64)
+            if have:
+                a_init(nxt)
+                x_codes(nxt)
+            k = 0
+            cb = None
+            todo = []
+
+            def ctx_quant(cg, cgt):
+                nc.vector.quantize_mx(
+                    out=cc[:, cg, px].bitcast(FP8X4),
+                    scales=cs[4 * cg : P, px],
+                    in_=cgt[:, px, :].rearrange("p x t -> p (x t)"),
+                )
+
+            for ct in range(16):
+                cg, t = divmod(ct, 4)
+                if have:
+                    x_copy(nxt, cg, t)
+                if t == 0:
+                    cb = cbp.tile([P, 4, 512], BF16, name="cb", tag="cb")
+                banded(plan, ct, cb, px)
+                if have:
+                    for i in range(4):
+                        a_op(nxt, k)
+                        k += 1
+                if len(todo) > 0:
+                    qcg, qt = todo.pop()
+                    ctx_quant(qcg, qt)
+                if t == 3:
+                    if have:
+                        x_quant(nxt, cg)
+                        if nxt + 1 < STRIPES:
+                            load_x(nxt + 1, cg)
+                    cgt = cgp.tile([P, 512, 4], BF16, name="cgt", tag="cgt", align_bytes=64)
+                    nc.vector.tensor_copy(
+                        out=cgt[:, px, :], in_=cb[:, :, px].rearrange("p t x -> p x t")
+                    )
+                    todo.append((cg, cgt))
+            if have:
+                for i in range(2):
+                    a_op(nxt, k)
+                    k += 1
+            qcg, qt = todo.pop()
+            ctx_quant(qcg, qt)
+            if have:
+                stage1(nxt)
+            for ot in range(16):
+                stage2(gam, ot, cc, cs, px)
+                if have:
+                    for i in range(3):
+                        if k < len(a_ops):
+                            a_op(nxt, k)
+                            k += 1

@@ -34,105 +34,18 @@ def tap_offsets():
 
 
 def band_plan(gam):
-    written = [[False] * IMG for r in range(TR)]
     parts = []
     if gam >= 0:
         parts.append((gam, 1, 0, 4 if gam % 8 == 7 else 8))
     if gam + 1 < STRIPES:
         parts.append((gam + 1, 0, 4 if (gam + 1) % 8 == 0 else 0, 8))
-    pieces = []
+    banks = ([], [])
     for (sg, half, r0, r1) in parts:
         for s in range(4):
             lo = max(0, TCOL * s - HALO)
             hi = min(IMG, TCOL * s + TCOL + HALO)
-            first = lo
-            for c in range(lo + 1, hi + 1):
-                if c == hi or written[r0][c] != written[r0][first]:
-                    pieces.append((sg, s, half, r0, r1, first, c))
-                    first = c
-            for r in range(r0, r1):
-                for cc in range(lo, hi):
-                    written[r][cc] = True
-    return pieces
-
-
-def prep_weight(nc, wst, pst, ident, w, permute, codes, planes):
-    for cg in range(4):
-        rows = w[512 * cg : 512 * (cg + 1), :]
-        wr = wst.tile([P, 4, 2048], BF16, name="wr", tag="wr")
-        if permute:
-            nc.sync.dma_start(out=wr[:], in_=rows.rearrange("(m t) k -> m t k", t=4))
-        else:
-            nc.sync.dma_start(out=wr[:], in_=rows.rearrange("(t m) k -> m t k", t=4))
-        words = wr[:].bitcast(F32)
-        for g in range(4):
-            grp = wst.tile([P, 512, 4], BF16, name="wg", tag="wg", align_bytes=64)
-            flat = grp[:].rearrange("p c j -> p (c j)")
-            gw = flat.bitcast(F32)
-            for h in range(2):
-                pt = pst.tile([P, 2, 2, P], F32, name="pt", tag="pt")
-                for tt in range(2):
-                    for u in range(2):
-                        nc.tensor.transpose(
-                            pt[:, tt, u, :],
-                            words[:, 2 * h + tt, 256 * g + u : 256 * (g + 1) : 2],
-                            ident[:],
-                        )
-                dst = gw[:, 512 * h : 512 * (h + 1)].rearrange("p (t m u) -> p t m u", t=2, u=2)
-                src = pt[:].rearrange("p t u m -> p t m u")
-                if h == 0:
-                    nc.vector.tensor_copy(out=dst, in_=src)
-                else:
-                    nc.scalar.copy(out=dst, in_=src)
-            cols = slice(512 * cg, 512 * (cg + 1))
-            nc.vector.quantize_mx(
-                out=codes[:, g, cols].bitcast(FP8X4),
-                scales=planes[4 * g : P, cols],
-                in_=flat,
-            )
-
-
-def prep_small(nc, pro, pst, ident, attn, v_b, w_b, taps, vbb, wbc):
-    ash = pro.tile([P, 2, IMG, IMG], BF16, name="ash")
-    nc.vector.memset(ash[:], 0.0)
-    for (n, dr, dc) in tap_offsets():
-        r0, r1 = max(0, dr), min(IMG, IMG + dr)
-        c0, c1 = max(0, dc), min(IMG, IMG + dc)
-        for b in range(2):
-            nc.scalar.dma_start(
-                out=ash[n : n + 1, b, r0:r1, c0:c1],
-                in_=attn[b, n : n + 1, r0 - dr : r1 - dr, c0 - dc : c1 - dc],
-            )
-    asp = pro.tile([P, 64, P], F32, name="asp")
-    for sg in range(STRIPES):
-        b, j = divmod(sg, 8)
-        nc.vector.tensor_copy(
-            out=asp[:, 4 * sg : 4 * sg + 4, :].rearrange("p s (r c) -> p s r c", c=TCOL),
-            in_=ash[:, b, TR * j : TR * (j + 1), :].rearrange("p r (s c) -> p s r c", c=TCOL),
-        )
-    for k in range(16):
-        pt = pst.tile([P, 4, P], F32, name="pt", tag="pt")
-        for i in range(4):
-            nc.tensor.transpose(pt[:, i, :], asp[:, 4 * k + i, :], ident[:])
-        nc.vector.tensor_copy(out=taps[:, 4 * k : 4 * k + 4, :], in_=pt[:, :, 0:NTAP])
-    nc.vector.tensor_tensor(out=taps[:, :, 4], in0=taps[:, :, 4], in1=taps[:, :, 13], op=ADD)
-    nc.vector.tensor_tensor(out=taps[:, :, 4], in0=taps[:, :, 4], in1=taps[:, :, 22], op=ADD)
-
-    vbr = pro.tile([P, 2048], BF16, name="vbr")
-    nc.sync.dma_start(out=vbr[:], in_=v_b.partition_broadcast(P))
-    nc.vector.tensor_copy(
-        out=vbb[:].rearrange("p (g t m) -> p g t m", g=4, t=4),
-        in_=vbr[:].rearrange("p (g m t) -> p g t m", g=4, t=4),
-    )
-
-    wbr = pro.tile([P, P], BF16, name="wbr")
-    nc.vector.memset(wbr[:], 0.0)
-    nc.sync.dma_start(out=wbr[0:16, :], in_=w_b.rearrange("(a m) -> a m", m=P))
-    wbf = pro.tile([P, P], F32, name="wbf")
-    nc.vector.tensor_copy(out=wbf[:], in_=wbr[:])
-    pt = pst.tile([P, 4, P], F32, name="pt", tag="pt")
-    nc.tensor.transpose(pt[:, 0, :], wbf[:], ident[:])
-    nc.vector.tensor_copy(out=wbc[:], in_=pt[:, 0, 0:16])
+            banks[s % 2].append((sg, s, half, r0, r1, lo, hi))
+    return banks
 
 
 def tile_selfattentionmodulev2_pb_l_kernel(tc, x, attn, v_w, v_b, w_w, w_b, out):
@@ -142,6 +55,11 @@ def tile_selfattentionmodulev2_pb_l_kernel(tc, x, attn, v_w, v_b, w_w, w_b, out)
         xrp = ctx.enter_context(tc.tile_pool(name="xrp", bufs=4))
         xgp = ctx.enter_context(tc.tile_pool(name="xgp", bufs=2))
         xcp = ctx.enter_context(tc.tile_pool(name="xcp", bufs=1))
+        vtp = ctx.enter_context(tc.tile_pool(name="vtp", bufs=8))
+        cgp = ctx.enter_context(tc.tile_pool(name="cgp", bufs=2))
+        psm = ctx.enter_context(tc.psum_pool(name="psm", bufs=4))
+        psb = ctx.enter_context(tc.psum_pool(name="psb", bufs=2))
+        ctx.enter_context(tc.manual_schedule())
 
         ident = const.tile([P, P], F32, name="ident")
         make_identity(nc, ident[:])
@@ -152,12 +70,18 @@ def tile_selfattentionmodulev2_pb_l_kernel(tc, x, attn, v_w, v_b, w_w, w_b, out)
         taps = const.tile([P, 64, NTAP], F32, name="taps")
         vbb = const.tile([P, 2048], F32, name="vbb")
         wbc = const.tile([P, 16], F32, name="wbc")
+        evens = []
+        for i in range(3):
+            ev = const.tile([P, TR, IMG], F32, name="ev%d" % i)
+            nc.gpsimd.memset(ev[:], 0.0)
+            evens.append(ev)
 
         xraw = {}
         xgrp = {}
         xcod = {}
         vts = {}
         ats = {}
+        chunks = {}
 
         def load_x(sg, g):
             b, j = divmod(sg, 8)
@@ -175,15 +99,15 @@ def tile_selfattentionmodulev2_pb_l_kernel(tc, x, attn, v_w, v_b, w_w, w_b, out)
             xs = xcp.tile([P, 512], U8, name="xs", tag="xs", align_bytes=64)
             xcod[sg] = (xc, xs)
 
-        def x_copy(sg, g, s):
+        def x_copy(sg, g, s, on_vector):
             if s == 0:
                 xgrp[(sg, g)] = xgp.tile([P, 512, 4], BF16, name="xg", tag="xg", align_bytes=64)
-            xg = xgrp[(sg, g)]
-            xr = xraw[(sg, g)]
-            nc.scalar.copy(
-                out=xg[:, P * s : P * (s + 1), :].rearrange("p (r c) i -> p r c i", c=TCOL),
-                in_=xr[:].rearrange("p i (r s c) -> p s r c i", s=4, c=TCOL)[:, s],
-            )
+            dst = xgrp[(sg, g)][:, P * s : P * (s + 1), :].rearrange("p (r c) i -> p r c i", c=TCOL)
+            src = xraw[(sg, g)][:].rearrange("p i (r s c) -> p s r c i", s=4, c=TCOL)[:, s]
+            if on_vector:
+                nc.vector.tensor_copy(out=dst, in_=src)
+            else:
+                nc.scalar.copy(out=dst, in_=src)
 
         def x_quant(sg, g):
             xc, xs = xcod[sg]
@@ -193,38 +117,71 @@ def tile_selfattentionmodulev2_pb_l_kernel(tc, x, attn, v_w, v_b, w_w, w_b, out)
                 in_=xgrp[(sg, g)][:].rearrange("p c i -> p (c i)"),
             )
 
-        with tc.tile_pool(name="pro", bufs=1) as pro:
-            with tc.tile_pool(name="wst", bufs=2) as wst:
-                with tc.psum_pool(name="pst", bufs=4) as pst:
-                    prep_small(nc, pro, pst, ident, attn, v_b, w_b, taps, vbb, wbc)
-                    prep_weight(nc, wst, pst, ident, v_w, True, vwc, vws)
-                    for g in range(4):
-                        load_x(0, g)
-                    prep_weight(nc, wst, pst, ident, w_w, False, wwc, wws)
+        def chunk_load(k):
+            if k >= 16:
+                return
+            w = v_w if k < 8 else w_w
+            cg, h = divmod(k % 8, 2)
+            rows = w[512 * cg : 512 * (cg + 1), :]
+            if k < 8:
+                view = rows.rearrange("(m t) k -> m t k", t=4)
+            else:
+                view = rows.rearrange("(t m) k -> m t k", t=4)
+            wr = vtp.tile([P, 2, 2048], BF16, name="wr", tag="vt")
+            nc.sync.dma_start(out=wr[:], in_=view[:, 2 * h : 2 * h + 2, :])
+            chunks[k] = wr
 
-        vtp = ctx.enter_context(tc.tile_pool(name="vtp", bufs=8))
-        atp = ctx.enter_context(tc.tile_pool(name="atp", bufs=12))
-        cbp = ctx.enter_context(tc.tile_pool(name="cbp", bufs=2))
-        cgp = ctx.enter_context(tc.tile_pool(name="cgp", bufs=2))
-        ccp = ctx.enter_context(tc.tile_pool(name="ccp", bufs=1))
-        obp = ctx.enter_context(tc.tile_pool(name="obp", bufs=4))
-        ps1 = ctx.enter_context(tc.psum_pool(name="ps1", bufs=3))
-        psb = ctx.enter_context(tc.psum_pool(name="psb", bufs=2))
-        ps2 = ctx.enter_context(tc.psum_pool(name="ps2", bufs=3))
+        def chunk_prep(k):
+            codes, planes = (vwc, vws) if k < 8 else (wwc, wws)
+            words = chunks[k][:].bitcast(F32)
+            cols = slice(256 * (k % 8), 256 * (k % 8 + 1))
+            for g in range(4):
+                pt = psm.tile([P, 2, 2, P], F32, name="pt", tag="mx")
+                for tt in range(2):
+                    for u in range(2):
+                        nc.tensor.transpose(
+                            pt[:, tt, u, :], words[:, tt, 256 * g + u : 256 * (g + 1) : 2], ident[:]
+                        )
+                grp = cgp.tile([P, 256, 4], BF16, name="wg", tag="cgt", align_bytes=64)
+                flat = grp[:].rearrange("p c j -> p (c j)")
+                dst = flat.bitcast(F32).rearrange("p (t m u) -> p t m u", t=2, u=2)
+                src = pt[:].rearrange("p t u m -> p t m u")
+                if k < 4 and g % 2 == 0:
+                    nc.vector.tensor_copy(out=dst, in_=src)
+                else:
+                    nc.scalar.copy(out=dst, in_=src)
+                nc.vector.quantize_mx(
+                    out=codes[:, g, cols].bitcast(FP8X4), scales=planes[4 * g : P, cols], in_=flat
+                )
+            chunk_load(k + 4)
+
+        def vt_alloc(sg):
+            for s in range(4):
+                vts[(sg, s)] = vtp.tile([P, 2048], F32, name="vt", tag="vt")
+
+        def stage1_bank(sg, s, cg):
+            xc, xs = xcod[sg]
+            px = slice(P * s, P * (s + 1))
+            cols = slice(512 * cg, 512 * (cg + 1))
+            ps = psm.tile([P, 512], F32, name="m1", tag="mx")
+            for g in range(4):
+                nc.tensor.matmul_mx(
+                    out=ps[:],
+                    lhsT=xc[:, g, px].bitcast(FP8X4),
+                    lhsT_scale=xs[4 * g : P, px],
+                    rhs=vwc[:, g, cols].bitcast(FP8X4),
+                    rhs_scale=vws[4 * g : P, cols],
+                    start=(g == 0),
+                    stop=(g == 3),
+                )
+            nc.vector.tensor_tensor(out=vts[(sg, s)][:, cols], in0=ps[:], in1=vbb[:, cols], op=ADD)
 
         a_ops = [(n, dr, dc, s) for (n, dr, dc) in tap_offsets() if n != 13 and n != 22 for s in range(4)]
         ident3 = ident[:].rearrange("p (r c) -> p r c", c=TCOL)
 
-        def a_init(sg):
-            for s in range(4):
-                at = atp.tile([P, 2 * TR, TCOL + 2 * HALO], F32, name="at", tag="at")
-                nc.gpsimd.memset(at[:], 0.0)
-                ats[(sg, s)] = at
-
         def a_op(sg, k):
             n, dr, dc, s = a_ops[k]
-            at = ats[(sg, s)]
-            win = at[:, HALO - dr : HALO - dr + TR, HALO - dc : HALO - dc + TCOL]
+            win = ats[(sg, s)][:, HALO - dr : HALO - dr + TR, HALO - dc : HALO - dc + TCOL]
             nc.vector.scalar_tensor_tensor(
                 out=win,
                 in0=ident3,
@@ -234,29 +191,79 @@ def tile_selfattentionmodulev2_pb_l_kernel(tc, x, attn, v_w, v_b, w_w, w_b, out)
                 op1=ADD,
             )
 
-        def stage1(sg):
-            xc, xs = xcod[sg]
-            for s in range(4):
-                vt = vtp.tile([P, 2048], F32, name="vt", tag="vt")
-                vts[(sg, s)] = vt
-                px = slice(P * s, P * (s + 1))
-                for cg in range(4):
-                    cols = slice(512 * cg, 512 * (cg + 1))
-                    ps = ps1.tile([P, 512], F32, name="s1", tag="s1")
-                    for g in range(4):
-                        nc.tensor.matmul_mx(
-                            out=ps[:],
-                            lhsT=xc[:, g, px].bitcast(FP8X4),
-                            lhsT_scale=xs[4 * g : P, px],
-                            rhs=vwc[:, g, cols].bitcast(FP8X4),
-                            rhs_scale=vws[4 * g : P, cols],
-                            start=(g == 0),
-                            stop=(g == 3),
-                        )
-                    nc.vector.tensor_tensor(out=vt[:, cols], in0=ps[:], in1=vbb[:, cols], op=ADD)
+        with tc.tile_pool(name="pro", bufs=1) as pro:
+            ash = pro.tile([P, 2, IMG * IMG], BF16, name="ash")
+            nc.vector.memset(ash[:], 0.0)
+            wbr = pro.tile([P, P], BF16, name="wbr")
+            nc.vector.memset(wbr[:], 0.0)
+            vbr = pro.tile([P, 2048], BF16, name="vbr")
+            asp = pro.tile([P, 64, P], BF16, name="asp")
+            identb = pro.tile([P, P], BF16, name="identb")
+            make_identity(nc, identb[:])
 
-        def banded(plan, ct, cb, px):
-            ps = psb.tile([P, TR, IMG], F32, name="bd", tag="bd")
+            for g in range(4):
+                load_x(0, g)
+            nc.sync.dma_start(out=vbr[:], in_=v_b.partition_broadcast(P))
+            for k in range(4):
+                chunk_load(k)
+            nc.sync.dma_start(out=wbr[0:16, :], in_=w_b.rearrange("(a m) -> a m", m=P))
+            flat_attn = attn.rearrange("b n h w -> n b (h w)")
+            for (n, dr, dc) in tap_offsets():
+                shift = dr * IMG + dc
+                lo = max(0, shift)
+                hi = IMG * IMG + min(0, shift)
+                nc.sync.dma_start(
+                    out=ash[n : n + 1, :, lo:hi], in_=flat_attn[n : n + 1, :, lo - shift : hi - shift]
+                )
+
+            x_codes(0)
+            for g in range(4):
+                for s in range(4):
+                    x_copy(0, g, s, g % 2 == 1)
+                x_quant(0, g)
+                load_x(1, g)
+            nc.vector.tensor_copy(
+                out=vbb[:].rearrange("p (g t m) -> p g t m", g=4, t=4),
+                in_=vbr[:].rearrange("p (g m t) -> p g t m", g=4, t=4),
+            )
+            vt_alloc(0)
+            chunk_prep(0)
+            chunk_prep(1)
+            for s in range(4):
+                stage1_bank(0, s, 0)
+            chunk_prep(2)
+            chunk_prep(3)
+            for sg in range(STRIPES):
+                b, j = divmod(sg, 8)
+                nc.scalar.copy(
+                    out=asp[:, 4 * sg : 4 * sg + 4, :].rearrange("p s (r c) -> p s r c", c=TCOL),
+                    in_=ash[:, b, 512 * j : 512 * (j + 1)].rearrange("p (r s c) -> p s r c", s=4, c=TCOL),
+                )
+            for s in range(4):
+                stage1_bank(0, s, 1)
+            for sg in range(STRIPES):
+                pt = psm.tile([P, 4, P], BF16, name="pa", tag="mx")
+                for s in range(4):
+                    nc.tensor.transpose(pt[:, s, :], asp[:, 4 * sg + s, :], identb[:])
+                nc.vector.tensor_copy(out=taps[:, 4 * sg : 4 * sg + 4, :], in_=pt[:, :, 0:NTAP])
+            pt = psm.tile([P, 4, P], BF16, name="pa", tag="mx")
+            nc.tensor.transpose(pt[:, 0, :], wbr[:], identb[:])
+            nc.vector.tensor_copy(out=wbc[:], in_=pt[:, 0, 0:16])
+            nc.vector.tensor_tensor(out=taps[:, :, 4], in0=taps[:, :, 4], in1=taps[:, :, 13], op=ADD)
+            nc.vector.tensor_tensor(out=taps[:, :, 4], in0=taps[:, :, 4], in1=taps[:, :, 22], op=ADD)
+
+        atp = ctx.enter_context(tc.tile_pool(name="atp", bufs=12))
+        cbp = ctx.enter_context(tc.tile_pool(name="cbp", bufs=2))
+        ccp = ctx.enter_context(tc.tile_pool(name="ccp", bufs=1))
+        obp = ctx.enter_context(tc.tile_pool(name="obp", bufs=4))
+
+        def a_init(sg):
+            for s in range(4):
+                at = atp.tile([P, 2 * TR, TCOL + 2 * HALO], F32, name="at", tag="at")
+                nc.gpsimd.memset(at[:], 0.0)
+                ats[(sg, s)] = at
+
+        def pieces(ps, plan, ct):
             last = len(plan) - 1
             for i, (sg, s, half, r0, r1, c0, c1) in enumerate(plan):
                 a0 = TCOL * s - HALO
@@ -267,7 +274,22 @@ def tile_selfattentionmodulev2_pb_l_kernel(tc, x, attn, v_w, v_b, w_w, w_b, out)
                     start=(i == 0),
                     stop=(i == last),
                 )
-            nc.scalar.copy(out=cb[:, ct % 4, px], in_=ps[:].rearrange("p r c -> p (r c)")[:, px])
+
+        def banded(plan, ct, cb, r0, r1):
+            ev = evens[ct % 3]
+            pe = psb.tile([P, TR, IMG], F32, name="be", tag="be")
+            pieces(pe, plan[0], ct)
+            nc.scalar.copy(out=ev[:, r0:r1, 0:20], in_=pe[:, r0:r1, 0:20])
+            nc.scalar.copy(out=ev[:, r0:r1, 28:52], in_=pe[:, r0:r1, 28:52])
+            po = psb.tile([P, TR, IMG], F32, name="bo", tag="bo")
+            pieces(po, plan[1], ct)
+            cbv = cb[:, ct % 4, :].rearrange("p (r c) -> p r c", c=IMG)
+            for (c0, c1) in ((12, 36), (44, 64)):
+                nc.vector.tensor_tensor(
+                    out=cbv[:, r0:r1, c0:c1], in0=po[:, r0:r1, c0:c1], in1=ev[:, r0:r1, c0:c1], op=ADD
+                )
+            for (c0, c1) in ((0, 12), (36, 44)):
+                nc.vector.tensor_copy(out=cbv[:, r0:r1, c0:c1], in_=ev[:, r0:r1, c0:c1])
 
         def store(gam, ot, ob):
             orow = slice(P * ot, P * (ot + 1))
@@ -290,7 +312,7 @@ def tile_selfattentionmodulev2_pb_l_kernel(tc, x, attn, v_w, v_b, w_w, w_b, out)
                     )
 
         def stage2(gam, ot, cc, cs, px):
-            ps = ps2.tile([P, 512], F32, name="s2", tag="s2")
+            ps = psm.tile([P, 512], F32, name="m2", tag="mx")
             ocol = slice(P * ot, P * (ot + 1))
             for g in range(4):
                 nc.tensor.matmul_mx(
@@ -308,18 +330,17 @@ def tile_selfattentionmodulev2_pb_l_kernel(tc, x, attn, v_w, v_b, w_w, w_b, out)
             )
             store(gam, ot, ob)
 
-        ctx.enter_context(tc.manual_schedule())
-
-        x_codes(0)
-        for g in range(4):
-            for s in range(4):
-                x_copy(0, g, s)
-            x_quant(0, g)
-            load_x(1, g)
         a_init(0)
-        for k in range(len(a_ops)):
-            a_op(0, k)
-        stage1(0)
+        k0 = 0
+        for k in range(4, 16):
+            chunk_prep(k)
+            for i in range(12 if k < 8 else 7):
+                if k0 < len(a_ops):
+                    a_op(0, k0)
+                    k0 += 1
+            if k == 5 or k == 7:
+                for s in range(4):
+                    stage1_bank(0, s, k // 2)
 
         for gam in range(-1, STRIPES):
             nxt = gam + 2
@@ -345,14 +366,14 @@ def tile_selfattentionmodulev2_pb_l_kernel(tc, x, attn, v_w, v_b, w_w, w_b, out)
             for ct in range(16):
                 cg, t = divmod(ct, 4)
                 if have:
-                    x_copy(nxt, cg, t)
+                    x_copy(nxt, cg, t, False)
                 if t == 0:
                     cb = cbp.tile([P, 4, 512], BF16, name="cb", tag="cb")
-                banded(plan, ct, cb, px)
                 if have:
                     for i in range(4):
                         a_op(nxt, k)
                         k += 1
+                banded(plan, ct, cb, 4 if gam < 0 else 0, 4 if gam == STRIPES - 1 else 8)
                 if len(todo) > 0:
                     qcg, qt = todo.pop()
                     ctx_quant(qcg, qt)
@@ -373,7 +394,10 @@ def tile_selfattentionmodulev2_pb_l_kernel(tc, x, attn, v_w, v_b, w_w, w_b, out)
             qcg, qt = todo.pop()
             ctx_quant(qcg, qt)
             if have:
-                stage1(nxt)
+                vt_alloc(nxt)
+                for s in range(4):
+                    for cg in range(4):
+                        stage1_bank(nxt, s, cg)
             for ot in range(16):
                 stage2(gam, ot, cc, cs, px)
                 if have:

@@ -59,7 +59,6 @@ def tile_selfattentionmodulev2_pb_l_kernel(tc, x, attn, v_w, v_b, w_w, w_b, out)
         cgp = ctx.enter_context(tc.tile_pool(name="cgp", bufs=2))
         psm = ctx.enter_context(tc.psum_pool(name="psm", bufs=4))
         psb = ctx.enter_context(tc.psum_pool(name="psb", bufs=2))
-        ctx.enter_context(tc.manual_schedule())
 
         ident = const.tile([P, P], F32, name="ident")
         make_identity(nc, ident[:])
@@ -342,13 +341,18 @@ def tile_selfattentionmodulev2_pb_l_kernel(tc, x, attn, v_w, v_b, w_w, w_b, out)
                 for s in range(4):
                     stage1_bank(0, s, k // 2)
 
+        late = []
         for gam in range(-1, STRIPES):
             nxt = gam + 2
             have = nxt < STRIPES
             plan = band_plan(gam)
             px = slice(256 if gam < 0 else 0, 256 if gam == STRIPES - 1 else 512)
-            cc = ccp.tile([P, 4, 512], U32, name="cc", tag="cc", align_bytes=64)
-            cs = ccp.tile([P, 512], U8, name="cs", tag="cs", align_bytes=64)
+            if gam < STRIPES - 1:
+                cc = ccp.tile([P, 4, 512], U32, name="cc", tag="cc", align_bytes=64)
+                cs = ccp.tile([P, 512], U8, name="cs", tag="cs", align_bytes=64)
+            else:
+                cc = xcp.tile([P, 4, 512], U32, name="cc", tag="xc", align_bytes=64)
+                cs = xcp.tile([P, 512], U8, name="cs", tag="xs", align_bytes=64)
             if have:
                 a_init(nxt)
                 x_codes(nxt)
@@ -363,6 +367,11 @@ def tile_selfattentionmodulev2_pb_l_kernel(tc, x, attn, v_w, v_b, w_w, w_b, out)
                     in_=cgt[:, px, :].rearrange("p x t -> p (x t)"),
                 )
 
+            def ctx_group(cg):
+                cgt = cgp.tile([P, 512, 4], BF16, name="cgt", tag="cgt", align_bytes=64)
+                nc.vector.tensor_copy(out=cgt[:, px, :], in_=cb[:, :, px].rearrange("p t x -> p x t"))
+                return cgt
+
             for ct in range(16):
                 cg, t = divmod(ct, 4)
                 if have:
@@ -373,35 +382,36 @@ def tile_selfattentionmodulev2_pb_l_kernel(tc, x, attn, v_w, v_b, w_w, w_b, out)
                     for i in range(4):
                         a_op(nxt, k)
                         k += 1
+                    if t == 3:
+                        x_quant(nxt, cg)
+                        if nxt + 1 < STRIPES:
+                            load_x(nxt + 1, cg)
                 banded(plan, ct, cb, 4 if gam < 0 else 0, 4 if gam == STRIPES - 1 else 8)
                 if len(todo) > 0:
                     qcg, qt = todo.pop()
                     ctx_quant(qcg, qt)
-                if t == 3:
-                    if have:
-                        x_quant(nxt, cg)
-                        if nxt + 1 < STRIPES:
-                            load_x(nxt + 1, cg)
-                    cgt = cgp.tile([P, 512, 4], BF16, name="cgt", tag="cgt", align_bytes=64)
-                    nc.vector.tensor_copy(
-                        out=cgt[:, px, :], in_=cb[:, :, px].rearrange("p t x -> p x t")
-                    )
-                    todo.append((cg, cgt))
-            if have:
-                for i in range(2):
-                    a_op(nxt, k)
-                    k += 1
-            qcg, qt = todo.pop()
-            ctx_quant(qcg, qt)
+                if t == 3 and cg < 3:
+                    todo.append((cg, ctx_group(cg)))
             if have:
                 vt_alloc(nxt)
                 for s in range(4):
                     for cg in range(4):
                         stage1_bank(nxt, s, cg)
-            for ot in range(16):
-                stage2(gam, ot, cc, cs, px)
-                if have:
-                    for i in range(3):
-                        if k < len(a_ops):
-                            a_op(nxt, k)
-                            k += 1
+                    if s == 0:
+                        cgt = ctx_group(3)
+                    if s == 1:
+                        ctx_quant(3, cgt)
+            else:
+                ctx_quant(3, ctx_group(3))
+            late.append((gam, cc, cs, px))
+            if gam == STRIPES - 2:
+                continue
+            for (lgam, lcc, lcs, lpx) in late:
+                for ot in range(16):
+                    stage2(lgam, ot, lcc, lcs, lpx)
+                    if have:
+                        for i in range(3):
+                            if k < len(a_ops):
+                                a_op(nxt, k)
+                                k += 1
+            late = []

@@ -59,6 +59,7 @@ def tile_selfattentionmodulev2_pb_l_kernel(tc, x, attn, v_w, v_b, w_w, w_b, out)
         cgp = ctx.enter_context(tc.tile_pool(name="cgp", bufs=2))
         psm = ctx.enter_context(tc.psum_pool(name="psm", bufs=4))
         psb = ctx.enter_context(tc.psum_pool(name="psb", bufs=2))
+        ctx.enter_context(tc.manual_schedule())
 
         ident = const.tile([P, P], F32, name="ident")
         make_identity(nc, ident[:])

from contextlib import ExitStack

import concourse.mybir as mybir
from concourse.masks import make_identity

FLOPS = 2 * 2 * 2048 * 2048 * 8192 + 2 * 27 * 2048 * 8192

F32 = mybir.dt.float32
BF16 = mybir.dt.bfloat16
U32 = mybir.dt.uint32
U8 = mybir.dt.uint8
FP8X4 = mybir.dt.float8_e4m3fn_x4
ADD = mybir.AluOpType.add
MULT = mybir.AluOpType.mult
IDENTITY = mybir.ActivationFunctionType.Identity

P = 128
IMG = 64
TR = 8
TCOL = 16
HALO = 4
STRIPES = 16
NTAP = 27


def tap_offsets():
    taps = []
    for n in range(NTAP):
        d = (1, 2, 4)[n // 9]
        dr = ((n % 9) // 3 - 1) * d
        dc = (n % 3 - 1) * d
        taps.append((n, dr, dc))
    return taps


def band_plan(gam):
    parts = []
    if gam >= 0:
        parts.append((gam, 1, 0, 4 if gam % 8 == 7 else 8))
    if gam + 1 < STRIPES:
        parts.append((gam + 1, 0, 4 if (gam + 1) % 8 == 0 else 0, 8))
    banks = ([], [])
    for (sg, half, r0, r1) in parts:
        for s in range(4):
            lo = max(0, TCOL * s - HALO)
            hi = min(IMG, TCOL * s + TCOL + HALO)
            banks[s % 2].append((sg, s, half, r0, r1, lo, hi))
    return banks


def tile_selfattentionmodulev2_pb_l_kernel(tc, x, attn, v_w, v_b, w_w, w_b, out):
    nc = tc.nc
    with ExitStack() as ctx:
        const = ctx.enter_context(tc.tile_pool(name="const", bufs=1))
        xrp = ctx.enter_context(tc.tile_pool(name="xrp", bufs=4))
        xgp = ctx.enter_context(tc.tile_pool(name="xgp", bufs=2))
        xcp = ctx.enter_context(tc.tile_pool(name="xcp", bufs=1))
        vtp = ctx.enter_context(tc.tile_pool(name="vtp", bufs=8))
        cgp = ctx.enter_context(tc.tile_pool(name="cgp", bufs=2))
        psm = ctx.enter_context(tc.psum_pool(name="psm", bufs=4))
        psb = ctx.enter_context(tc.psum_pool(name="psb", bufs=2))
        ctx.enter_context(tc.manual_schedule())

        ident = const.tile([P, P], F32, name="ident")
        make_identity(nc, ident[:])
        vwc = const.tile([P, 4, 2048], U32, name="vwc", align_bytes=64)
        vws = const.tile([P, 2048], U8, name="vws", align_bytes=64)
        wwc = const.tile([P, 4, 2048], U32, name="wwc", align_bytes=64)
        wws = const.tile([P, 2048], U8, name="wws", align_bytes=64)
        taps = const.tile([P, 64, NTAP], F32, name="taps")
        vbb = const.tile([P, 2048], F32, name="vbb")
        wbc = const.tile([P, 16], F32, name="wbc")
        evens = []
        for i in range(3):
            ev = const.tile([P, TR, IMG], F32, name="ev%d" % i)
            nc.gpsimd.memset(ev[:], 0.0)
            evens.append(ev)

        xraw = {}
        xgrp = {}
        xcod = {}
        vts = {}
        ats = {}
        chunks = {}

        def load_x(sg, g):
            b, j = divmod(sg, 8)
            xr = xrp.tile([P, 4, 512], BF16, name="xr", tag="xr")
            nc.sync.dma_start(
                out=xr[:],
                in_=x[b, 512 * g : 512 * (g + 1), TR * j : TR * (j + 1), :].rearrange(
                    "(p i) h w -> p i (h w)", i=4
                ),
            )
            xraw[(sg, g)] = xr

        def x_codes(sg):
            xc = xcp.tile([P, 4, 512], U32, name="xc", tag="xc", align_bytes=64)
            xs = xcp.tile([P, 512], U8, name="xs", tag="xs", align_bytes=64)
            xcod[sg] = (xc, xs)

        def x_copy(sg, g, s, on_vector):
            if s == 0:
                xgrp[(sg, g)] = xgp.tile([P, 512, 4], BF16, name="xg", tag="xg", align_bytes=64)
            dst = xgrp[(sg, g)][:, P * s : P * (s + 1), :].rearrange("p (r c) i -> p r c i", c=TCOL)
            src = xraw[(sg, g)][:].rearrange("p i (r s c) -> p s r c i", s=4, c=TCOL)[:, s]
            if on_vector:
                nc.vector.tensor_copy(out=dst, in_=src)
            else:
                nc.scalar.copy(out=dst, in_=src)

        def x_quant(sg, g):
            xc, xs = xcod[sg]
            nc.vector.quantize_mx(
                out=xc[:, g, :].bitcast(FP8X4),
                scales=xs[4 * g : P, :],
                in_=xgrp[(sg, g)][:].rearrange("p c i -> p (c i)"),
            )

        def chunk_load(k):
            if k >= 16:
                return
            w = v_w if k < 8 else w_w
            cg, h = divmod(k % 8, 2)
            rows = w[512 * cg : 512 * (cg + 1), :]
            if k < 8:
                view = rows.rearrange("(m t) k -> m t k", t=4)
            else:
                view = rows.rearrange("(t m) k -> m t k", t=4)
            wr = vtp.tile([P, 2, 2048], BF16, name="wr", tag="vt")
            nc.sync.dma_start(out=wr[:], in_=view[:, 2 * h : 2 * h + 2, :])
            chunks[k] = wr

        def chunk_prep(k):
            codes, planes = (vwc, vws) if k < 8 else (wwc, wws)
            words = chunks[k][:].bitcast(F32)
            cols = slice(256 * (k % 8), 256 * (k % 8 + 1))
            for g in range(4):
                pt = psm.tile([P, 2, 2, P], F32, name="pt", tag="mx")
                for tt in range(2):
                    for u in range(2):
                        nc.tensor.transpose(
                            pt[:, tt, u, :], words[:, tt, 256 * g + u : 256 * (g + 1) : 2], ident[:]
                        )
                grp = cgp.tile([P, 256, 4], BF16, name="wg", tag="cgt", align_bytes=64)
                flat = grp[:].rearrange("p c j -> p (c j)")
                dst = flat.bitcast(F32).rearrange("p (t m u) -> p t m u", t=2, u=2)
                src = pt[:].rearrange("p t u m -> p t m u")
                if k < 4 and g % 2 == 0:
                    nc.vector.tensor_copy(out=dst, in_=src)
                else:
                    nc.scalar.copy(out=dst, in_=src)
                nc.vector.quantize_mx(
                    out=codes[:, g, cols].bitcast(FP8X4), scales=planes[4 * g : P, cols], in_=flat
                )
            chunk_load(k + 4)

        def vt_alloc(sg):
            for s in range(4):
                vts[(sg, s)] = vtp.tile([P, 2048], F32, name="vt", tag="vt")

        def stage1_bank(sg, s, cg):
            xc, xs = xcod[sg]
            px = slice(P * s, P * (s + 1))
            cols = slice(512 * cg, 512 * (cg + 1))
            ps = psm.tile([P, 512], F32, name="m1", tag="mx")
            for g in range(4):
                nc.tensor.matmul_mx(
                    out=ps[:],
                    lhsT=xc[:, g, px].bitcast(FP8X4),
                    lhsT_scale=xs[4 * g : P, px],
                    rhs=vwc[:, g, cols].bitcast(FP8X4),
                    rhs_scale=vws[4 * g : P, cols],
                    start=(g == 0),
                    stop=(g == 3),
                )
            nc.vector.tensor_tensor(out=vts[(sg, s)][:, cols], in0=ps[:], in1=vbb[:, cols], op=ADD)

        a_ops = [(n, dr, dc, s) for (n, dr, dc) in tap_offsets() if n != 13 and n != 22 for s in range(4)]
        ident3 = ident[:].rearrange("p (r c) -> p r c", c=TCOL)

        def a_op(sg, k):
            n, dr, dc, s = a_ops[k]
            win = ats[(sg, s)][:, HALO - dr : HALO - dr + TR, HALO - dc : HALO - dc + TCOL]
            nc.vector.scalar_tensor_tensor(
                out=win,
                in0=ident3,
                scalar=taps[:, 4 * sg + s, n : n + 1],
                in1=win,
                op0=MULT,
                op1=ADD,
            )

        with tc.tile_pool(name="pro", bufs=1) as pro:
            ash = pro.tile([P, 2, IMG * IMG], BF16, name="ash")
            nc.vector.memset(ash[:], 0.0)
            wbr = pro.tile([P, P], BF16, name="wbr")
            nc.vector.memset(wbr[:], 0.0)
            vbr = pro.tile([P, 2048], BF16, name="vbr")
            asp = pro.tile([P, 64, P], BF16, name="asp")
            identb = pro.tile([P, P], BF16, name="identb")
            make_identity(nc, identb[:])

            for g in range(4):
                load_x(0, g)
            nc.sync.dma_start(out=vbr[:], in_=v_b.partition_broadcast(P))
            for k in range(4):
                chunk_load(k)
            nc.sync.dma_start(out=wbr[0:16, :], in_=w_b.rearrange("(a m) -> a m", m=P))
            flat_attn = attn.rearrange("b n h w -> n b (h w)")
            for (n, dr, dc) in tap_offsets():
                shift = dr * IMG + dc
                lo = max(0, shift)
                hi = IMG * IMG + min(0, shift)
                nc.sync.dma_start(
                    out=ash[n : n + 1, :, lo:hi], in_=flat_attn[n : n + 1, :, lo - shift : hi - shift]
                )

            x_codes(0)
            for g in range(4):
                for s in range(4):
                    x_copy(0, g, s, g % 2 == 1)
                x_quant(0, g)
                load_x(1, g)
            nc.vector.tensor_copy(
                out=vbb[:].rearrange("p (g t m) -> p g t m", g=4, t=4),
                in_=vbr[:].rearrange("p (g m t) -> p g t m", g=4, t=4),
            )
            vt_alloc(0)
            chunk_prep(0)
            chunk_prep(1)
            for s in range(4):
                stage1_bank(0, s, 0)
            chunk_prep(2)
            chunk_prep(3)
            for sg in range(STRIPES):
                b, j = divmod(sg, 8)
                nc.scalar.copy(
                    out=asp[:, 4 * sg : 4 * sg + 4, :].rearrange("p s (r c) -> p s r c", c=TCOL),
                    in_=ash[:, b, 512 * j : 512 * (j + 1)].rearrange("p (r s c) -> p s r c", s=4, c=TCOL),
                )
            for s in range(4):
                stage1_bank(0, s, 1)
            for sg in range(STRIPES):
                pt = psm.tile([P, 4, P], BF16, name="pa", tag="mx")
                for s in range(4):
                    nc.tensor.transpose(pt[:, s, :], asp[:, 4 * sg + s, :], identb[:])
                nc.vector.tensor_copy(out=taps[:, 4 * sg : 4 * sg + 4, :], in_=pt[:, :, 0:NTAP])
            pt = psm.tile([P, 4, P], BF16, name="pa", tag="mx")
            nc.tensor.transpose(pt[:, 0, :], wbr[:], identb[:])
            nc.vector.tensor_copy(out=wbc[:], in_=pt[:, 0, 0:16])
            nc.vector.tensor_tensor(out=taps[:, :, 4], in0=taps[:, :, 4], in1=taps[:, :, 13], op=ADD)
            nc.vector.tensor_tensor(out=taps[:, :, 4], in0=taps[:, :, 4], in1=taps[:, :, 22], op=ADD)

        atp = ctx.enter_context(tc.tile_pool(name="atp", bufs=12))
        cbp = ctx.enter_context(tc.tile_pool(name="cbp", bufs=2))
        ccp = ctx.enter_context(tc.tile_pool(name="ccp", bufs=1))
        obp = ctx.enter_context(tc.tile_pool(name="obp", bufs=4))

        def a_init(sg):
            for s in range(4):
                at = atp.tile([P, 2 * TR, TCOL + 2 * HALO], F32, name="at", tag="at")
                nc.gpsimd.memset(at[:], 0.0)
                ats[(sg, s)] = at

        def pieces(ps, plan, ct):
            last = len(plan) - 1
            for i, (sg, s, half, r0, r1, c0, c1) in enumerate(plan):
                a0 = TCOL * s - HALO
                nc.tensor.matmul(
                    out=ps[:, r0:r1, c0:c1],
                    lhsT=vts[(sg, s)][:, P * ct : P * (ct + 1)],
                    rhs=ats[(sg, s)][:, TR * half + r0 : TR * half + r1, c0 - a0 : c1 - a0],
                    start=(i == 0),
                    stop=(i == last),
                )

        def banded(plan, ct, cb, r0, r1):
            ev = evens[ct % 3]
            pe = psb.tile([P, TR, IMG], F32, name="be", tag="be")
            pieces(pe, plan[0], ct)
            nc.scalar.copy(out=ev[:, r0:r1, 0:20], in_=pe[:, r0:r1, 0:20])
            nc.scalar.copy(out=ev[:, r0:r1, 28:52], in_=pe[:, r0:r1, 28:52])
            po = psb.tile([P, TR, IMG], F32, name="bo", tag="bo")
            pieces(po, plan[1], ct)
            cbv = cb[:, ct % 4, :].rearrange("p (r c) -> p r c", c=IMG)
            for (c0, c1) in ((12, 36), (44, 64)):
                nc.vector.tensor_tensor(
                    out=cbv[:, r0:r1, c0:c1], in0=po[:, r0:r1, c0:c1], in1=ev[:, r0:r1, c0:c1], op=ADD
                )
            for (c0, c1) in ((0, 12), (36, 44)):
                nc.vector.tensor_copy(out=cbv[:, r0:r1, c0:c1], in_=ev[:, r0:r1, c0:c1])

        def store(gam, ot, ob):
            orow = slice(P * ot, P * (ot + 1))
            if gam >= 0 and gam % 8 != 7:
                b, j = divmod(gam, 8)
                nc.sync.dma_start(
                    out=out[b, orow, TR * j + 4 : TR * j + 12, :].rearrange("o h w -> o (h w)"),
                    in_=ob[:],
                )
            else:
                if gam >= 0:
                    nc.sync.dma_start(
                        out=out[gam // 8, orow, IMG - 4 : IMG, :].rearrange("o h w -> o (h w)"),
                        in_=ob[:, 0:256],
                    )
                if gam + 1 < STRIPES:
                    nc.sync.dma_start(
                        out=out[(gam + 1) // 8, orow, 0:4, :].rearrange("o h w -> o (h w)"),
                        in_=ob[:, 256:512],
                    )

        def stage2(gam, ot, cc, cs, px):
            ps = psm.tile([P, 512], F32, name="m2", tag="mx")
            ocol = slice(P * ot, P * (ot + 1))
            for g in range(4):
                nc.tensor.matmul_mx(
                    out=ps[:, px],
                    lhsT=wwc[:, g, ocol].bitcast(FP8X4),
                    lhsT_scale=wws[4 * g : P, ocol],
                    rhs=cc[:, g, px].bitcast(FP8X4),
                    rhs_scale=cs[4 * g : P, px],
                    start=(g == 0),
                    stop=(g == 3),
                )
            ob = obp.tile([P, 512], F32, name="ob", tag="ob")
            nc.scalar.activation(
                out=ob[:, px], in_=ps[:, px], func=IDENTITY, bias=wbc[:, ot : ot + 1], scale=1.0
            )
            store(gam, ot, ob)

        a_init(0)
        k0 = 0
        for k in range(4, 16):
            chunk_prep(k)
            for i in range(12 if k < 8 else 7):
                if k0 < len(a_ops):
                    a_op(0, k0)
                    k0 += 1
            if k == 5 or k == 7:
                for s in range(4):
                    stage1_bank(0, s, k // 2)

        late = []
        for gam in range(-1, STRIPES):
            nxt = gam + 2
            have = nxt < STRIPES
            plan = band_plan(gam)
            px = slice(256 if gam < 0 else 0, 256 if gam == STRIPES - 1 else 512)
            if gam < STRIPES - 1:
                cc = ccp.tile([P, 4, 512], U32, name="cc", tag="cc", align_bytes=64)
                cs = ccp.tile([P, 512], U8, name="cs", tag="cs", align_bytes=64)
            else:
                cc = xcp.tile([P, 4, 512], U32, name="cc", tag="xc", align_bytes=64)
                cs = xcp.tile([P, 512], U8, name="cs", tag="xs", align_bytes=64)
            if have:
                a_init(nxt)
                x_codes(nxt)
            k = 0
            cb = None
            todo = []

            def ctx_quant(cg, cgt):
                nc.vector.quantize_mx(
                    out=cc[:, cg, px].bitcast(FP8X4),
                    scales=cs[4 * cg : P, px],
                    in_=cgt[:, px, :].rearrange("p x t -> p (x t)"),
                )

            def ctx_group(cg):
                cgt = cgp.tile([P, 512, 4], BF16, name="cgt", tag="cgt", align_bytes=64)
                nc.vector.tensor_copy(out=cgt[:, px, :], in_=cb[:, :, px].rearrange("p t x -> p x t"))
                return cgt

            for ct in range(16):
                cg, t = divmod(ct, 4)
                if have:
                    x_copy(nxt, cg, t, False)
                if t == 0:
                    cb = cbp.tile([P, 4, 512], BF16, name="cb", tag="cb")
                if have:
                    for i in range(4):
                        a_op(nxt, k)
                        k += 1
                    if t == 3:
                        x_quant(nxt, cg)
                        if nxt + 1 < STRIPES:
                            load_x(nxt + 1, cg)
                banded(plan, ct, cb, 4 if gam < 0 else 0, 4 if gam == STRIPES - 1 else 8)
                if len(todo) > 0:
                    qcg, qt = todo.pop()
                    ctx_quant(qcg, qt)
                if t == 3 and cg < 3:
                    todo.append((cg, ctx_group(cg)))
            if have:
                vt_alloc(nxt)
                for s in range(4):
                    for cg in range(4):
                        stage1_bank(nxt, s, cg)
                    if s == 0:
                        cgt = ctx_group(3)
                    if s == 1:
                        ctx_quant(3, cgt)
            else:
                ctx_quant(3, ctx_group(3))
            late.append((gam, cc, cs, px))
            if gam == STRIPES - 2:
                continue
            for (lgam, lcc, lcs, lpx) in late:
                for ot in range(16):
                    stage2(lgam, ot, lcc, lcs, lpx)
                    if have:
                        for i in range(3):
                            if k < len(a_ops):
                                a_op(nxt, k)
                                k += 1
            late = []
